import numpy as np
import ml_dtypes


BF16 = ml_dtypes.bfloat16


def bf(x):
    return np.asarray(x, np.float32).astype(BF16)


def f64(x):
    return np.asarray(x).astype(np.float64)


E2M1 = np.array([0.0, 0.5, 1.0, 1.5, 2.0, 3.0, 4.0, 6.0, -0.0, -0.5, -1.0, -1.5, -2.0, -3.0, -4.0, -6.0])


def pack_weight(w, fmt):
    k, n = w.shape
    w = f64(bf(w)).reshape(k // 32, 32, n)
    amax = np.abs(w).max(1)
    if fmt == "e4m3":
        byte = np.frexp(amax)[1] - 1 + 127 - 7
    else:
        mant, ex = np.frexp(amax / 6.0)
        byte = np.where(mant > 0.5, ex, ex - 1) + 127
    byte = np.clip(np.where(amax > 0, byte, 1), 1, 254)
    scaled = (w * np.exp2(127.0 - byte)[:, None, :]).reshape(k, n).astype(np.float32)
    by_word = np.ascontiguousarray(scaled.reshape(k // 512, 128, 4, n).transpose(0, 1, 3, 2))
    if fmt == "e4m3":
        words = by_word.astype(ml_dtypes.float8_e4m3fn).view(np.uint8)
    else:
        c = by_word.astype(ml_dtypes.float4_e2m1fn).view(np.uint8) & 0xF
        words = c[..., 0::2] | (c[..., 1::2] << 4)
    return np.ascontiguousarray(words), np.ascontiguousarray(byte.astype(np.uint8).reshape(k // 512, 16, n))


def unpack_weight(words, scales, fmt):
    g, p, n, _ = words.shape
    if fmt == "e4m3":
        vals = np.ascontiguousarray(words).view(ml_dtypes.float8_e4m3fn).astype(np.float64)
    else:
        nib = np.empty((g, p, n, 4), np.uint8)
        nib[..., 0::2] = words & 0xF
        nib[..., 1::2] = words >> 4
        vals = E2M1[nib]
    vals = vals * np.repeat(np.exp2(scales.astype(np.float64) - 127.0), 8, axis=1)[..., None]
    return vals.transpose(0, 1, 3, 2).reshape(g * 512, n)

def pack4(w):
    words, scales = pack_weight(w, "e2m1")
    return words.reshape(words.shape[0], 128, -1), scales


def unpack4(words, scales):
    return unpack_weight(words.reshape(words.shape[0], 128, -1, 2), scales, "e2m1")


def kspread(k):
    return np.exp2(np.repeat(np.random.randint(-6, 7, k // 32), 32).astype(np.float64))


B, T, D, H, QB = 1, 128, 3584, 8, 64
DH = D // H
HP = H // 2
EPS = 1e-6
ROPE_BASE = 10000.0


def rmsnorm(u):
    return u / np.sqrt(np.mean(u * u, axis=-1, keepdims=True) + EPS)


def rope_tables():
    inv_freq = 1.0 / ROPE_BASE ** (np.arange(0, DH, 2) / DH)
    freqs = np.arange(T)[:, None] * inv_freq[None, :]
    return np.cos(freqs), np.sin(freqs)


def apply_rotary(u, cos, sin):
    d = DH // 2
    u1, u2 = u[..., :d], u[..., d:]
    c = cos[None, :, None, :]
    s = sin[None, :, None, :]
    return np.concatenate([u1 * c + u2 * s, -u1 * s + u2 * c], axis=-1)


def setup_inputs():
    s = kspread(D)
    hidden_states = np.random.standard_normal((B, T, D)) * s
    hidden_states_words, hidden_states_scales = pack4(np.ascontiguousarray(hidden_states.reshape(B * T, D).T))
    words, scales = pack4(np.random.standard_normal((D, 3 * D)) / np.sqrt(D) / s[:, None])
    return {"hidden_states_words": hidden_states_words,
            "hidden_states_scales": hidden_states_scales,
            "W_qkv_words": words,
            "W_qkv_scales": scales}


def reference(hidden_states_words, hidden_states_scales, W_qkv_words, W_qkv_scales):
    x = unpack4(hidden_states_words, hidden_states_scales).T
    qkv = x @ unpack4(W_qkv_words, W_qkv_scales)
    qkv = qkv.reshape(B, T, H, 3 * DH)
    q = qkv[..., :DH]
    k = qkv[..., DH:2 * DH]
    v = qkv[..., 2 * DH:]
    v = v.reshape(B, T, HP, 2 * DH)
    cos, sin = rope_tables()
    q = apply_rotary(rmsnorm(q), cos, sin)
    k = apply_rotary(rmsnorm(k), cos, sin)
    return q, k, v

@@ -1,0 +1,266 @@
+from contextlib import ExitStack
+
+import concourse.mybir as mybir
+
+F32 = mybir.dt.float32
+I32 = mybir.dt.int32
+U8 = mybir.dt.uint8
+FP4X4 = mybir.dt.float4_e2m1fn_x4
+ALU = mybir.AluOpType
+ACT = mybir.ActivationFunctionType
+
+P = 128
+G = 7
+HEADS = 8
+DH = 448
+HALF = DH // 2
+HEAD_COLS = 3 * DH
+COLS = HEADS * HEAD_COLS
+WIN = 512
+PAIR_COLS = 2 * HEAD_COLS
+TILE_BYTES = 2 * PAIR_COLS
+W_BUFS = 16
+EPS = 1e-6
+ROPE_BASE = 10000.0
+
+FLOPS = 2 * 128 * 3584 * 10752
+
+PI = 3.141592653589793
+TWO_PI_HI = 6.28125
+TWO_PI_LO = 2.0 * PI - TWO_PI_HI
+
+
+def make_plan():
+    units = []
+    jobs = []
+    for pair in range(3):
+        first = len(units)
+        for g in range(G):
+            units.append((pair * PAIR_COLS, PAIR_COLS, (g,)))
+        for a in range(2):
+            h = 2 * pair + a
+            hc = h * HEAD_COLS
+            where = {}
+            for g in range(G):
+                where[g] = (first + g, 0)
+            jobs.append((h, (("q", hc, 0), ("k", hc + DH, 0), ("v", hc + HEAD_COLS - WIN, WIN - DH)), where))
+
+    def add(h, c0, width, groups, segs):
+        where = {}
+        for gs in groups:
+            for slot, g in enumerate(gs):
+                where[g] = (len(units), slot)
+            units.append((c0, width, gs))
+        jobs.append((h, segs, where))
+
+    hc = 6 * HEAD_COLS
+    add(6, hc, HEAD_COLS, ((0, 1), (2, 3), (4, 5), (6,)),
+        (("q", hc, 0), ("k", hc + DH, 0), ("v", hc + HEAD_COLS - WIN, WIN - DH)))
+    hc = 7 * HEAD_COLS
+    add(7, hc, 2 * DH, ((0, 1, 2), (3, 4, 5), (6,)),
+        (("q", hc, 0), ("k", hc + 2 * DH - WIN, WIN - DH)))
+    add(7, hc + HEAD_COLS - WIN, WIN, ((0, 1, 2, 3), (4, 5), (6,)),
+        (("v", hc + HEAD_COLS - WIN, WIN - DH),))
+    return units, jobs
+
+
+def tile_mixerdiffattention_pa_kernel(tc, x_words, x_scales, w_words, w_scales, out_0, out_1, out_2):
+    nc = tc.nc
+    units, jobs = make_plan()
+    last_use = {}
+    for j, job in enumerate(jobs):
+        for g in range(G):
+            last_use[job[2][g][0]] = (j, g)
+    outs = {
+        "q": out_0.rearrange("b t h d -> (b t) (h d)"),
+        "k": out_1.rearrange("b t h d -> (b t) (h d)"),
+        "v": out_2.rearrange("b t h d -> (b t) (h d)"),
+    }
+
+    with ExitStack() as ctx:
+        ctx.enter_context(tc.manual_schedule())
+        keep = ctx.enter_context(tc.tile_pool(name="keep", bufs=1))
+        wpool = ctx.enter_context(tc.tile_pool(name="wpool", bufs=W_BUFS))
+        small = ctx.enter_context(tc.tile_pool(name="small", bufs=4))
+        rot = ctx.enter_context(tc.tile_pool(name="rot", bufs=4))
+        outp = ctx.enter_context(tc.tile_pool(name="outp", bufs=2))
+        psum = ctx.enter_context(tc.psum_pool(name="psum", bufs=8))
+
+        xc = keep.tile([P, G, 2 * P], U8, name="xc", align_bytes=64)
+        xs = keep.tile([P, G, P], U8, name="xs", align_bytes=64)
+        planes0 = keep.tile([P, G, PAIR_COLS], U8, name="planes0", align_bytes=64)
+        planes_rest = []
+        for g in range(G):
+            pr = keep.tile([P, COLS - PAIR_COLS], U8, name="planes_rest%d" % g, align_bytes=64)
+            planes_rest.append(pr)
+
+        def scale_window(g, wc):
+            if wc < PAIR_COLS:
+                return planes0[:, g, wc : wc + WIN]
+            return planes_rest[g][:, wc - PAIR_COLS : wc - PAIR_COLS + WIN]
+
+        tiles = {}
+        state = {"next": 0, "live": 0}
+
+        def load_unit(u):
+            c0, width, gs = units[u]
+            nb = 2 * width
+            t = wpool.tile([P, TILE_BYTES], U8, name="wt", tag="wt", align_bytes=64)
+            if len(gs) == 1:
+                nc.sync.dma_start(
+                    out=t[:, 0:nb].bitcast(I32),
+                    in_=w_words[gs[0], :, 2 * c0 : 2 * c0 + nb].bitcast(I32),
+                )
+            else:
+                nc.sync.dma_start(
+                    out=t[:, 0 : len(gs) * nb].rearrange("p (g n) -> p g n", g=len(gs)).bitcast(I32),
+                    in_=w_words[gs[0] : gs[-1] + 1, :, 2 * c0 : 2 * c0 + nb].rearrange("g p n -> p g n").bitcast(I32),
+                )
+            tiles[u] = t
+
+        def top_up(limit):
+            while state["next"] < len(units) and state["live"] < limit:
+                load_unit(state["next"])
+                state["next"] += 1
+                state["live"] += 1
+
+        nc.sync.dma_start(out=xc[:].bitcast(I32), in_=x_words.rearrange("g p n -> p g n").bitcast(I32))
+        top_up(G)
+
+        nc.vector.memset(xs[:].rearrange("p g n -> p (g n)").bitcast(I32), 0)
+        nc.vector.memset(planes0[:].rearrange("p g n -> p (g n)").bitcast(I32), 0)
+        for g in range(G):
+            nc.vector.memset(planes_rest[g][:].bitcast(I32), 0)
+
+        for r in range(4):
+            nc.sync.dma_start(
+                out=xs[r:P:32, :, :].bitcast(I32),
+                in_=x_scales[:, r:16:4, :].rearrange("g q n -> q g n").bitcast(I32),
+            )
+        for r in range(4):
+            nc.sync.dma_start(
+                out=planes0[r:P:32, :, :].bitcast(I32),
+                in_=w_scales[:, r:16:4, 0:PAIR_COLS].rearrange("g q n -> q g n").bitcast(I32),
+            )
+        for g in range(G):
+            for r in range(4):
+                nc.sync.dma_start(
+                    out=planes_rest[g][r:P:32, :].bitcast(I32),
+                    in_=w_scales[g, r:16:4, PAIR_COLS:COLS].bitcast(I32),
+                )
+        top_up(W_BUFS)
+
+        pos_i = keep.tile([P, 1], I32, name="pos_i")
+        nc.gpsimd.iota(pos_i[:], pattern=[[0, 1]], base=0, channel_multiplier=1)
+        pos = keep.tile([P, 1], F32, name="pos")
+        nc.vector.tensor_copy(out=pos[:], in_=pos_i[:])
+        eps = keep.tile([P, 1], F32, name="eps")
+        nc.vector.memset(eps[:], EPS)
+        freq = keep.tile([P, HALF], F32, name="freq")
+        nc.vector.memset(freq[:, 0:1], 1.0)
+        n = 1
+        while n < HALF:
+            m = min(n, HALF - n)
+            nc.vector.tensor_scalar(out=freq[:, n : n + m], in0=freq[:, 0:m],
+                                    scalar1=ROPE_BASE ** (-2.0 * n / DH), scalar2=None, op0=ALU.mult)
+            n *= 2
+        ang = keep.tile([P, DH], F32, name="ang")
+        nc.vector.tensor_scalar(out=ang[:, 0:HALF], in0=freq[:], scalar1=pos[:], scalar2=0.5 * PI,
+                                op0=ALU.mult, op1=ALU.add)
+        nc.vector.tensor_scalar(out=ang[:, HALF:DH], in0=freq[:], scalar1=pos[:], scalar2=None, op0=ALU.mult)
+        turns_i = keep.tile([P, DH], I32, name="turns_i")
+        nc.vector.tensor_scalar(out=turns_i[:], in0=ang[:], scalar1=0.5 / PI, scalar2=None, op0=ALU.mult)
+        turns = keep.tile([P, DH], F32, name="turns")
+        nc.vector.tensor_copy(out=turns[:], in_=turns_i[:])
+        red1 = keep.tile([P, DH], F32, name="red1")
+        nc.vector.scalar_tensor_tensor(out=red1[:], in0=turns[:], scalar=-TWO_PI_HI, in1=ang[:], op0=ALU.mult, op1=ALU.add)
+        red2 = keep.tile([P, DH], F32, name="red2")
+        nc.vector.scalar_tensor_tensor(out=red2[:], in0=turns[:], scalar=-TWO_PI_LO, in1=red1[:], op0=ALU.mult, op1=ALU.add)
+        over = keep.tile([P, DH], F32, name="over")
+        nc.vector.tensor_scalar(out=over[:], in0=red2[:], scalar1=PI, scalar2=None, op0=ALU.is_gt)
+        red3 = keep.tile([P, DH], F32, name="red3")
+        nc.vector.scalar_tensor_tensor(out=red3[:], in0=over[:], scalar=-2.0 * PI, in1=red2[:], op0=ALU.mult, op1=ALU.add)
+        under = keep.tile([P, DH], F32, name="under")
+        nc.vector.tensor_scalar(out=under[:], in0=red3[:], scalar1=-PI, scalar2=None, op0=ALU.is_lt)
+        red4 = keep.tile([P, DH], F32, name="red4")
+        nc.vector.scalar_tensor_tensor(out=red4[:], in0=under[:], scalar=2.0 * PI, in1=red3[:], op0=ALU.mult, op1=ALU.add)
+        cos2 = keep.tile([P, DH], F32, name="cos2")
+        sin2 = keep.tile([P, DH], F32, name="sin2")
+        nc.scalar.activation(out=cos2[:, 0:HALF], in_=red4[:, 0:HALF], func=ACT.Sin)
+        nc.scalar.activation(out=cos2[:, HALF:DH], in_=red4[:, 0:HALF], func=ACT.Sin)
+        nc.scalar.activation(out=sin2[:, 0:HALF], in_=red4[:, HALF:DH], func=ACT.Sin)
+        nc.scalar.activation(out=sin2[:, HALF:DH], in_=red4[:, HALF:DH], func=ACT.Sin, scale=-1.0)
+        warm = keep.tile([P, 1], F32, name="warm")
+        nc.scalar.activation(out=warm[:], in_=eps[:], func=ACT.Sqrt)
+        junk = keep.tile([P, DH], F32, name="junk")
+
+        open_out = {}
+
+        def norm_rope(parts):
+            ss = small.tile([P, 2], F32, name="ss", tag="ss")
+            for i, (bank, off, dst) in enumerate(parts):
+                nc.scalar.activation(out=junk[:], in_=bank[:, off : off + DH], func=ACT.Square,
+                                     accum_out=ss[:, i : i + 1])
+            std = small.tile([P, 2], F32, name="std", tag="std")
+            nc.scalar.activation(out=std[:], in_=ss[:], func=ACT.Sqrt, bias=eps[:], scale=1.0 / DH)
+            rstd = small.tile([P, 2], F32, name="rstd", tag="rstd")
+            nc.vector.reciprocal(out=rstd[:], in_=std[:])
+            prods = []
+            for i, (bank, off, dst) in enumerate(parts):
+                rs = rstd[:, i : i + 1]
+                at = rot.tile([P, DH], F32, name="at", tag="at")
+                bt = rot.tile([P, DH], F32, name="bt", tag="bt")
+                nc.vector.scalar_tensor_tensor(out=at[:], in0=bank[:, off : off + DH], scalar=rs, in1=cos2[:],
+                                               op0=ALU.mult, op1=ALU.mult)
+                nc.vector.scalar_tensor_tensor(out=bt[:, 0:HALF], in0=bank[:, off + HALF : off + DH], scalar=rs,
+                                               in1=sin2[:, 0:HALF], op0=ALU.mult, op1=ALU.mult)
+                nc.vector.scalar_tensor_tensor(out=bt[:, HALF:DH], in0=bank[:, off : off + HALF], scalar=rs,
+                                               in1=sin2[:, HALF:DH], op0=ALU.mult, op1=ALU.mult)
+                prods.append((at, bt))
+            for (bank, off, dst), (at, bt) in zip(parts, prods):
+                nc.vector.tensor_tensor(out=dst, in0=at[:], in1=bt[:], op=ALU.add)
+
+        for j, (h, segs, where) in enumerate(jobs):
+            banks = []
+            for seg in segs:
+                acc = psum.tile([P, WIN], F32, name="acc", tag="acc")
+                banks.append(acc)
+            for g in range(G):
+                u, slot = where[g]
+                c0, width, gs = units[u]
+                for (kind, wc, off), bank in zip(segs, banks):
+                    b0 = 2 * (slot * width + wc - c0)
+                    nc.tensor.matmul_mx(
+                        out=bank[:],
+                        lhsT=xc[:, g, :].bitcast(FP4X4),
+                        lhsT_scale=xs[:, g, :],
+                        rhs=tiles[u][:, b0 : b0 + 2 * WIN].bitcast(FP4X4),
+                        rhs_scale=scale_window(g, wc),
+                        start=(g == 0),
+                        stop=(g == G - 1),
+                    )
+                if last_use[u] == (j, g):
+                    state["live"] -= 1
+                    top_up(W_BUFS)
+
+            paired = h < 6
+            side = h % 2 if paired else 0
+            dsts = {}
+            for kind, wc, off in segs:
+                if side == 0:
+                    ot = outp.tile([P, 2 * DH], F32, name="o" + kind, tag="o" + kind)
+                    open_out[kind] = ot
+                dsts[kind] = open_out[kind][:, side * DH : (side + 1) * DH]
+            by_kind = {}
+            for (kind, wc, off), bank in zip(segs, banks):
+                by_kind[kind] = (bank, off, dsts[kind])
+            if "q" in by_kind:
+                norm_rope((by_kind["q"], by_kind["k"]))
+            if "v" in by_kind:
+                bank, off, dst = by_kind["v"]
+                nc.scalar.copy(out=dst, in_=bank[:, off : off + DH])
+            for kind, wc, off in segs:
+                if paired and side == 1:
+                    nc.gpsimd.dma_start(out=outs[kind][:, (h - 1) * DH : (h + 1) * DH], in_=open_out[kind][:])
+                elif not paired:
+                    nc.sync.dma_start(out=outs[kind][:, h * DH : (h + 1) * DH], in_=open_out[kind][:, 0:DH])

@@ -23,6 +23,8 @@ W_BUFS = 16
 EPS = 1e-6
 ROPE_BASE = 10000.0
 
+KIND_COL = {"q": 0, "k": DH, "v": 2 * DH}
+
 FLOPS = 2 * 128 * 3584 * 10752
 
 PI = 3.141592653589793
@@ -30,37 +32,37 @@ TWO_PI_HI = 6.28125
 TWO_PI_LO = 2.0 * PI - TWO_PI_HI
 
 
+def window(seg0, lo, hi):
+    if seg0 + WIN <= hi:
+        return seg0, 0
+    assert seg0 + DH - WIN >= lo
+    return seg0 + DH - WIN, WIN - DH
+
+
 def make_plan():
     units = []
     jobs = []
-    for pair in range(3):
-        first = len(units)
-        for g in range(G):
-            units.append((pair * PAIR_COLS, PAIR_COLS, (g,)))
-        for a in range(2):
-            h = 2 * pair + a
-            hc = h * HEAD_COLS
-            where = {}
-            for g in range(G):
-                where[g] = (first + g, 0)
-            jobs.append((h, (("q", hc, 0), ("k", hc + DH, 0), ("v", hc + HEAD_COLS - WIN, WIN - DH)), where))
 
-    def add(h, c0, width, groups, segs):
+    def add(c0, width, groups, parts):
         where = {}
         for gs in groups:
             for slot, g in enumerate(gs):
                 where[g] = (len(units), slot)
             units.append((c0, width, gs))
-        jobs.append((h, segs, where))
+        segs = []
+        for kind, h in parts:
+            wc, off = window(h * HEAD_COLS + KIND_COL[kind], c0, c0 + width)
+            segs.append((kind, h, wc, off))
+        jobs.append((tuple(segs), where))
 
-    hc = 6 * HEAD_COLS
-    add(6, hc, HEAD_COLS, ((0, 1), (2, 3), (4, 5), (6,)),
-        (("q", hc, 0), ("k", hc + DH, 0), ("v", hc + HEAD_COLS - WIN, WIN - DH)))
-    hc = 7 * HEAD_COLS
-    add(7, hc, 2 * DH, ((0, 1, 2), (3, 4, 5), (6,)),
-        (("q", hc, 0), ("k", hc + 2 * DH - WIN, WIN - DH)))
-    add(7, hc + HEAD_COLS - WIN, WIN, ((0, 1, 2, 3), (4, 5), (6,)),
-        (("v", hc + HEAD_COLS - WIN, WIN - DH),))
+    single = tuple((g,) for g in range(G))
+    for pair in range(3):
+        a = 2 * pair
+        add(pair * PAIR_COLS, PAIR_COLS, single,
+            (("q", a), ("k", a), ("v", a), ("v", a + 1), ("q", a + 1), ("k", a + 1)))
+    add(6 * HEAD_COLS, HEAD_COLS, ((0, 1), (2, 3), (4, 5), (6,)), (("q", 6), ("k", 6), ("v", 6)))
+    add(7 * HEAD_COLS, 2 * DH, ((0, 1, 2), (3, 4, 5), (6,)), (("q", 7), ("k", 7)))
+    add(COLS - WIN, WIN, ((0, 1, 2, 3), (4, 5), (6,)), (("v", 7),))
     return units, jobs
 
 
@@ -70,7 +72,7 @@ def tile_mixerdiffattention_pa_kernel(tc, x_words, x_scales, w_words, w_scales, 
     last_use = {}
     for j, job in enumerate(jobs):
         for g in range(G):
-            last_use[job[2][g][0]] = (j, g)
+            last_use[job[1][g][0]] = (j, g)
     outs = {
         "q": out_0.rearrange("b t h d -> (b t) (h d)"),
         "k": out_1.rearrange("b t h d -> (b t) (h d)"),
@@ -81,10 +83,10 @@ def tile_mixerdiffattention_pa_kernel(tc, x_words, x_scales, w_words, w_scales, 
         ctx.enter_context(tc.manual_schedule())
         keep = ctx.enter_context(tc.tile_pool(name="keep", bufs=1))
         wpool = ctx.enter_context(tc.tile_pool(name="wpool", bufs=W_BUFS))
-        small = ctx.enter_context(tc.tile_pool(name="small", bufs=4))
-        rot = ctx.enter_context(tc.tile_pool(name="rot", bufs=4))
+        small = ctx.enter_context(tc.tile_pool(name="small", bufs=8))
+        rot = ctx.enter_context(tc.tile_pool(name="rot", bufs=6))
         outp = ctx.enter_context(tc.tile_pool(name="outp", bufs=2))
-        psum = ctx.enter_context(tc.psum_pool(name="psum", bufs=8))
+        psum = ctx.enter_context(tc.psum_pool(name="psum", bufs=1))
 
         xc = keep.tile([P, G, 2 * P], U8, name="xc", align_bytes=64)
         xs = keep.tile([P, G, P], U8, name="xs", align_bytes=64)
@@ -100,7 +102,7 @@ def tile_mixerdiffattention_pa_kernel(tc, x_words, x_scales, w_words, w_scales, 
             return planes_rest[g][:, wc - PAIR_COLS : wc - PAIR_COLS + WIN]
 
         tiles = {}
-        state = {"next": 0, "live": 0}
+        state = {"next": 0, "live": 0, "banks_used": 0}
 
         def load_unit(u):
             c0, width, gs = units[u]
@@ -125,12 +127,10 @@ def tile_mixerdiffattention_pa_kernel(tc, x_words, x_scales, w_words, w_scales, 
                 state["live"] += 1
 
         nc.sync.dma_start(out=xc[:].bitcast(I32), in_=x_words.rearrange("g p n -> p g n").bitcast(I32))
-        top_up(G)
+        top_up(2)
 
         nc.vector.memset(xs[:].rearrange("p g n -> p (g n)").bitcast(I32), 0)
         nc.vector.memset(planes0[:].rearrange("p g n -> p (g n)").bitcast(I32), 0)
-        for g in range(G):
-            nc.vector.memset(planes_rest[g][:].bitcast(I32), 0)
 
         for r in range(4):
             nc.sync.dma_start(
@@ -142,13 +142,7 @@ def tile_mixerdiffattention_pa_kernel(tc, x_words, x_scales, w_words, w_scales, 
                 out=planes0[r:P:32, :, :].bitcast(I32),
                 in_=w_scales[:, r:16:4, 0:PAIR_COLS].rearrange("g q n -> q g n").bitcast(I32),
             )
-        for g in range(G):
-            for r in range(4):
-                nc.sync.dma_start(
-                    out=planes_rest[g][r:P:32, :].bitcast(I32),
-                    in_=w_scales[g, r:16:4, PAIR_COLS:COLS].bitcast(I32),
-                )
-        top_up(W_BUFS)
+        top_up(G)
 
         pos_i = keep.tile([P, 1], I32, name="pos_i")
         nc.gpsimd.iota(pos_i[:], pattern=[[0, 1]], base=0, channel_multiplier=1)
@@ -194,44 +188,31 @@ def tile_mixerdiffattention_pa_kernel(tc, x_words, x_scales, w_words, w_scales, 
         nc.scalar.activation(out=warm[:], in_=eps[:], func=ACT.Sqrt)
         junk = keep.tile([P, DH], F32, name="junk")
 
-        open_out = {}
+        for g in range(G):
+            nc.vector.memset(planes_rest[g][:].bitcast(I32), 0)
+        for g in range(G):
+            for r in range(4):
+                nc.sync.dma_start(
+                    out=planes_rest[g][r:P:32, :].bitcast(I32),
+                    in_=w_scales[g, r:16:4, PAIR_COLS:COLS].bitcast(I32),
+                )
 
-        def norm_rope(parts):
-            ss = small.tile([P, 2], F32, name="ss", tag="ss")
-            for i, (bank, off, dst) in enumerate(parts):
-                nc.scalar.activation(out=junk[:], in_=bank[:, off : off + DH], func=ACT.Square,
-                                     accum_out=ss[:, i : i + 1])
-            std = small.tile([P, 2], F32, name="std", tag="std")
-            nc.scalar.activation(out=std[:], in_=ss[:], func=ACT.Sqrt, bias=eps[:], scale=1.0 / DH)
-            rstd = small.tile([P, 2], F32, name="rstd", tag="rstd")
-            nc.vector.reciprocal(out=rstd[:], in_=std[:])
-            prods = []
-            for i, (bank, off, dst) in enumerate(parts):
-                rs = rstd[:, i : i + 1]
-                at = rot.tile([P, DH], F32, name="at", tag="at")
-                bt = rot.tile([P, DH], F32, name="bt", tag="bt")
-                nc.vector.scalar_tensor_tensor(out=at[:], in0=bank[:, off : off + DH], scalar=rs, in1=cos2[:],
-                                               op0=ALU.mult, op1=ALU.mult)
-                nc.vector.scalar_tensor_tensor(out=bt[:, 0:HALF], in0=bank[:, off + HALF : off + DH], scalar=rs,
-                                               in1=sin2[:, 0:HALF], op0=ALU.mult, op1=ALU.mult)
-                nc.vector.scalar_tensor_tensor(out=bt[:, HALF:DH], in0=bank[:, off : off + HALF], scalar=rs,
-                                               in1=sin2[:, HALF:DH], op0=ALU.mult, op1=ALU.mult)
-                prods.append((at, bt))
-            for (bank, off, dst), (at, bt) in zip(parts, prods):
-                nc.vector.tensor_tensor(out=dst, in0=at[:], in1=bt[:], op=ALU.add)
+        free_banks = list(range(8))
 
-        for j, (h, segs, where) in enumerate(jobs):
+        for j, (segs, where) in enumerate(jobs):
             banks = []
             for seg in segs:
-                acc = psum.tile([P, WIN], F32, name="acc", tag="acc")
-                banks.append(acc)
+                b = free_banks[state["banks_used"]]
+                state["banks_used"] += 1
+                acc = psum.tile([P, WIN], F32, name="bank%d" % b, tag="bank%d" % b)
+                banks.append((b, acc))
             for g in range(G):
                 u, slot = where[g]
                 c0, width, gs = units[u]
-                for (kind, wc, off), bank in zip(segs, banks):
+                for (kind, h, wc, off), (b, acc) in zip(segs, banks):
                     b0 = 2 * (slot * width + wc - c0)
                     nc.tensor.matmul_mx(
-                        out=bank[:],
+                        out=acc[:],
                         lhsT=xc[:, g, :].bitcast(FP4X4),
                         lhsT_scale=xs[:, g, :],
                         rhs=tiles[u][:, b0 : b0 + 2 * WIN].bitcast(FP4X4),
@@ -241,26 +222,58 @@ def tile_mixerdiffattention_pa_kernel(tc, x_words, x_scales, w_words, w_scales, 
                     )
                 if last_use[u] == (j, g):
                     state["live"] -= 1
-                    top_up(W_BUFS)
+                    if j > 0:
+                        top_up(W_BUFS)
 
-            paired = h < 6
-            side = h % 2 if paired else 0
-            dsts = {}
-            for kind, wc, off in segs:
-                if side == 0:
-                    ot = outp.tile([P, 2 * DH], F32, name="o" + kind, tag="o" + kind)
-                    open_out[kind] = ot
-                dsts[kind] = open_out[kind][:, side * DH : (side + 1) * DH]
-            by_kind = {}
-            for (kind, wc, off), bank in zip(segs, banks):
-                by_kind[kind] = (bank, off, dsts[kind])
-            if "q" in by_kind:
-                norm_rope((by_kind["q"], by_kind["k"]))
-            if "v" in by_kind:
-                bank, off, dst = by_kind["v"]
-                nc.scalar.copy(out=dst, in_=bank[:, off : off + DH])
-            for kind, wc, off in segs:
-                if paired and side == 1:
-                    nc.gpsimd.dma_start(out=outs[kind][:, (h - 1) * DH : (h + 1) * DH], in_=open_out[kind][:])
-                elif not paired:
-                    nc.sync.dma_start(out=outs[kind][:, h * DH : (h + 1) * DH], in_=open_out[kind][:, 0:DH])
+            heads = {}
+            for kind, h, wc, off in segs:
+                heads.setdefault(kind, []).append(h)
+            otiles = {}
+            for kind in heads:
+                ot = outp.tile([P, 2 * DH], F32, name="o" + kind, tag="o" + kind)
+                otiles[kind] = ot
+
+            rstds = {}
+            for (kind, h, wc, off), (b, acc) in zip(segs, banks):
+                dst = otiles[kind][:, (h - heads[kind][0]) * DH : (h - heads[kind][0] + 1) * DH]
+                if kind == "v":
+                    nc.scalar.copy(out=dst, in_=acc[:, off : off + DH])
+                else:
+                    ss = small.tile([P, 1], F32, name="ss", tag="ss")
+                    nc.scalar.activation(out=junk[:], in_=acc[:, off : off + DH], func=ACT.Square, accum_out=ss[:])
+                    std = small.tile([P, 1], F32, name="std", tag="std")
+                    nc.scalar.activation(out=std[:], in_=ss[:], func=ACT.Sqrt, bias=eps[:], scale=1.0 / DH)
+                    rstds[(kind, h)] = std
+            prods = []
+            for (kind, h, wc, off), (b, acc) in zip(segs, banks):
+                if kind == "v":
+                    continue
+                dst = otiles[kind][:, (h - heads[kind][0]) * DH : (h - heads[kind][0] + 1) * DH]
+                rs = small.tile([P, 1], F32, name="rs", tag="rs")
+                nc.vector.reciprocal(out=rs[:], in_=rstds[(kind, h)][:])
+                at = rot.tile([P, DH], F32, name="at", tag="at")
+                bt = rot.tile([P, DH], F32, name="bt", tag="bt")
+                nc.vector.scalar_tensor_tensor(out=at[:], in0=acc[:, off : off + DH], scalar=rs[:], in1=cos2[:],
+                                               op0=ALU.mult, op1=ALU.mult)
+                nc.vector.scalar_tensor_tensor(out=bt[:, 0:HALF], in0=acc[:, off + HALF : off + DH], scalar=rs[:],
+                                               in1=sin2[:, 0:HALF], op0=ALU.mult, op1=ALU.mult)
+                nc.vector.scalar_tensor_tensor(out=bt[:, HALF:DH], in0=acc[:, off : off + HALF], scalar=rs[:],
+                                               in1=sin2[:, HALF:DH], op0=ALU.mult, op1=ALU.mult)
+                prods.append((dst, at, bt))
+            for dst, at, bt in prods:
+                nc.vector.tensor_tensor(out=dst, in0=at[:], in1=bt[:], op=ALU.add)
+            for want_v in (True, False):
+                for (kind, h, wc, off), (b, acc) in zip(segs, banks):
+                    if (kind == "v") == want_v:
+                        free_banks.append(b)
+            if j == 0:
+                for kind in heads:
+                    for i, h in enumerate(heads[kind]):
+                        nc.sync.dma_start(out=outs[kind][:, h * DH : (h + 1) * DH], in_=otiles[kind][:, i * DH : (i + 1) * DH])
+                top_up(W_BUFS)
+            else:
+                for kind in heads:
+                    h0 = heads[kind][0]
+                    n_h = len(heads[kind])
+                    queue = nc.gpsimd if n_h == 2 else nc.sync
+                    queue.dma_start(out=outs[kind][:, h0 * DH : (h0 + n_h) * DH], in_=otiles[kind][:, 0 : n_h * DH])

@@ -91,15 +91,20 @@ def tile_mixerdiffattention_pa_kernel(tc, x_words, x_scales, w_words, w_scales, 
         xc = keep.tile([P, G, 2 * P], U8, name="xc", align_bytes=64)
         xs = keep.tile([P, G, P], U8, name="xs", align_bytes=64)
         planes0 = keep.tile([P, G, PAIR_COLS], U8, name="planes0", align_bytes=64)
-        planes_rest = []
-        for g in range(G):
-            pr = keep.tile([P, COLS - PAIR_COLS], U8, name="planes_rest%d" % g, align_bytes=64)
-            planes_rest.append(pr)
+        planes_rest = keep.tile([P, G, COLS - PAIR_COLS], U8, name="planes_rest", align_bytes=64)
 
         def scale_window(g, wc):
             if wc < PAIR_COLS:
                 return planes0[:, g, wc : wc + WIN]
-            return planes_rest[g][:, wc - PAIR_COLS : wc - PAIR_COLS + WIN]
+            return planes_rest[:, g, wc - PAIR_COLS : wc - PAIR_COLS + WIN]
+
+        def load_w_scales(dst, col0, col1):
+            for first in range(8):
+                p = 32 * (first // 4) + first % 4
+                nc.sync.dma_start(
+                    out=dst[p:P:64, :, :].bitcast(I32),
+                    in_=w_scales[:, first:16:8, col0:col1].rearrange("g q n -> q g n").bitcast(I32),
+                )
 
         tiles = {}
         state = {"next": 0, "live": 0, "banks_used": 0}
@@ -126,21 +131,15 @@ def tile_mixerdiffattention_pa_kernel(tc, x_words, x_scales, w_words, w_scales, 
                 state["next"] += 1
                 state["live"] += 1
 
-        nc.sync.dma_start(out=xc[:].bitcast(I32), in_=x_words.rearrange("g p n -> p g n").bitcast(I32))
         top_up(2)
-
-        nc.vector.memset(xs[:].rearrange("p g n -> p (g n)").bitcast(I32), 0)
         nc.vector.memset(planes0[:].rearrange("p g n -> p (g n)").bitcast(I32), 0)
-
+        nc.vector.memset(xs[:].rearrange("p g n -> p (g n)").bitcast(I32), 0)
+        load_w_scales(planes0, 0, PAIR_COLS)
+        nc.sync.dma_start(out=xc[:].bitcast(I32), in_=x_words.rearrange("g p n -> p g n").bitcast(I32))
         for r in range(4):
             nc.sync.dma_start(
                 out=xs[r:P:32, :, :].bitcast(I32),
                 in_=x_scales[:, r:16:4, :].rearrange("g q n -> q g n").bitcast(I32),
-            )
-        for r in range(4):
-            nc.sync.dma_start(
-                out=planes0[r:P:32, :, :].bitcast(I32),
-                in_=w_scales[:, r:16:4, 0:PAIR_COLS].rearrange("g q n -> q g n").bitcast(I32),
             )
         top_up(G)
 
@@ -188,14 +187,8 @@ def tile_mixerdiffattention_pa_kernel(tc, x_words, x_scales, w_words, w_scales, 
         nc.scalar.activation(out=warm[:], in_=eps[:], func=ACT.Sqrt)
         junk = keep.tile([P, DH], F32, name="junk")
 
-        for g in range(G):
-            nc.vector.memset(planes_rest[g][:].bitcast(I32), 0)
-        for g in range(G):
-            for r in range(4):
-                nc.sync.dma_start(
-                    out=planes_rest[g][r:P:32, :].bitcast(I32),
-                    in_=w_scales[g, r:16:4, PAIR_COLS:COLS].bitcast(I32),
-                )
+        nc.vector.memset(planes_rest[:].rearrange("p g n -> p (g n)").bitcast(I32), 0)
+        load_w_scales(planes_rest, PAIR_COLS, COLS)
 
         free_banks = list(range(8))
 
@@ -267,9 +260,9 @@ def tile_mixerdiffattention_pa_kernel(tc, x_words, x_scales, w_words, w_scales, 
                     if (kind == "v") == want_v:
                         free_banks.append(b)
             if j == 0:
-                for kind in heads:
-                    for i, h in enumerate(heads[kind]):
-                        nc.sync.dma_start(out=outs[kind][:, h * DH : (h + 1) * DH], in_=otiles[kind][:, i * DH : (i + 1) * DH])
+                for kind, cuts in (("v", (0, DH, DH + HALF, 2 * DH)), ("q", (0, DH, 2 * DH)), ("k", (0, DH, 2 * DH))):
+                    for lo, hi in zip(cuts[:-1], cuts[1:]):
+                        nc.sync.dma_start(out=outs[kind][:, lo:hi], in_=otiles[kind][:, lo:hi])
                 top_up(W_BUFS)
             else:
                 for kind in heads:

@@ -7,62 +7,61 @@ I32 = mybir.dt.int32
 U8 = mybir.dt.uint8
 FP4X4 = mybir.dt.float4_e2m1fn_x4
 ALU = mybir.AluOpType
-ACT = mybir.ActivationFunctionType
+FUNC = mybir.ActivationFunctionType
 
 P = 128
-G = 7
+PASSES = 7
 HEADS = 8
-DH = 448
-HALF = DH // 2
-HEAD_COLS = 3 * DH
-COLS = HEADS * HEAD_COLS
-WIN = 512
+SEGMENT = 448
+HALF = SEGMENT // 2
+SEGMENT_COL = {"q": 0, "k": SEGMENT, "v": 2 * SEGMENT}
+HEAD_COLS = 3 * SEGMENT
 PAIR_COLS = 2 * HEAD_COLS
-TILE_BYTES = 2 * PAIR_COLS
-W_BUFS = 16
+COLS = HEADS * HEAD_COLS
+WINDOW = 512
+UNIT_BYTES = 2 * PAIR_COLS
+LIVE_UNITS = 16
+PSUM_BANKS = 8
 EPS = 1e-6
 ROPE_BASE = 10000.0
 
-KIND_COL = {"q": 0, "k": DH, "v": 2 * DH}
+PI = 3.141592653589793
+TWO_PI_HIGH = 6.28125
+TWO_PI_LOW = 2.0 * PI - TWO_PI_HIGH
 
 FLOPS = 2 * 128 * 3584 * 10752
 
-PI = 3.141592653589793
-TWO_PI_HI = 6.28125
-TWO_PI_LO = 2.0 * PI - TWO_PI_HI
 
-
-def window(seg0, lo, hi):
-    if seg0 + WIN <= hi:
-        return seg0, 0
-    assert seg0 + DH - WIN >= lo
-    return seg0 + DH - WIN, WIN - DH
+def window_of(first_col, low, high):
+    if first_col + WINDOW <= high:
+        return first_col, 0
+    assert first_col + SEGMENT - WINDOW >= low
+    return first_col + SEGMENT - WINDOW, WINDOW - SEGMENT
 
 
 def make_plan():
     units = []
     jobs = []
 
-    def add(c0, width, groups, parts):
+    def add_job(first_col, width, pass_groups, parts):
         where = {}
-        for gs in groups:
-            for slot, g in enumerate(gs):
-                where[g] = (len(units), slot)
-            units.append((c0, width, gs))
-        segs = []
-        for kind, h in parts:
-            wc, off = window(h * HEAD_COLS + KIND_COL[kind], c0, c0 + width)
-            segs.append((kind, h, wc, off))
-        jobs.append((tuple(segs), where))
+        for group in pass_groups:
+            for place, g in enumerate(group):
+                where[g] = (len(units), place)
+            units.append((first_col, width, group))
+        segments = []
+        for kind, head in parts:
+            win, valid = window_of(head * HEAD_COLS + SEGMENT_COL[kind], first_col, first_col + width)
+            segments.append((kind, head, win, valid))
+        jobs.append((tuple(segments), where))
 
-    single = tuple((g,) for g in range(G))
-    for pair in range(3):
-        a = 2 * pair
-        add(pair * PAIR_COLS, PAIR_COLS, single,
-            (("q", a), ("k", a), ("v", a), ("v", a + 1), ("q", a + 1), ("k", a + 1)))
-    add(6 * HEAD_COLS, HEAD_COLS, ((0, 1), (2, 3), (4, 5), (6,)), (("q", 6), ("k", 6), ("v", 6)))
-    add(7 * HEAD_COLS, 2 * DH, ((0, 1, 2), (3, 4, 5), (6,)), (("q", 7), ("k", 7)))
-    add(COLS - WIN, WIN, ((0, 1, 2, 3), (4, 5), (6,)), (("v", 7),))
+    one_by_one = tuple((g,) for g in range(PASSES))
+    for a in (0, 2, 4):
+        add_job(a * HEAD_COLS, PAIR_COLS, one_by_one,
+                (("q", a), ("k", a), ("v", a), ("v", a + 1), ("q", a + 1), ("k", a + 1)))
+    add_job(6 * HEAD_COLS, HEAD_COLS, ((0, 1), (2, 3), (4, 5), (6,)), (("q", 6), ("k", 6), ("v", 6)))
+    add_job(7 * HEAD_COLS, 2 * SEGMENT, ((0, 1, 2), (3, 4, 5), (6,)), (("q", 7), ("k", 7)))
+    add_job(COLS - WINDOW, WINDOW, ((0, 1, 2, 3), (4, 5), (6,)), (("v", 7),))
     return units, jobs
 
 
@@ -70,9 +69,9 @@ def tile_mixerdiffattention_pa_kernel(tc, x_words, x_scales, w_words, w_scales, 
     nc = tc.nc
     units, jobs = make_plan()
     last_use = {}
-    for j, job in enumerate(jobs):
-        for g in range(G):
-            last_use[job[1][g][0]] = (j, g)
+    for j, (segments, where) in enumerate(jobs):
+        for g in range(PASSES):
+            last_use[where[g][0]] = (j, g)
     outs = {
         "q": out_0.rearrange("b t h d -> (b t) (h d)"),
         "k": out_1.rearrange("b t h d -> (b t) (h d)"),
@@ -82,191 +81,197 @@ def tile_mixerdiffattention_pa_kernel(tc, x_words, x_scales, w_words, w_scales, 
     with ExitStack() as ctx:
         ctx.enter_context(tc.manual_schedule())
         keep = ctx.enter_context(tc.tile_pool(name="keep", bufs=1))
-        wpool = ctx.enter_context(tc.tile_pool(name="wpool", bufs=W_BUFS))
-        small = ctx.enter_context(tc.tile_pool(name="small", bufs=8))
-        rot = ctx.enter_context(tc.tile_pool(name="rot", bufs=6))
-        outp = ctx.enter_context(tc.tile_pool(name="outp", bufs=2))
+        code_pool = ctx.enter_context(tc.tile_pool(name="code_pool", bufs=LIVE_UNITS))
+        stat_pool = ctx.enter_context(tc.tile_pool(name="stat_pool", bufs=8))
+        product_pool = ctx.enter_context(tc.tile_pool(name="product_pool", bufs=6))
+        out_pool = ctx.enter_context(tc.tile_pool(name="out_pool", bufs=2))
         psum = ctx.enter_context(tc.psum_pool(name="psum", bufs=1))
 
-        xc = keep.tile([P, G, 2 * P], U8, name="xc", align_bytes=64)
-        xs = keep.tile([P, G, P], U8, name="xs", align_bytes=64)
-        planes0 = keep.tile([P, G, PAIR_COLS], U8, name="planes0", align_bytes=64)
-        planes_rest = keep.tile([P, G, COLS - PAIR_COLS], U8, name="planes_rest", align_bytes=64)
+        x_codes = keep.tile([P, PASSES, 2 * P], U8, name="x_codes", align_bytes=64)
+        x_planes = keep.tile([P, PASSES, P], U8, name="x_planes", align_bytes=64)
+        w_planes_first = keep.tile([P, PASSES, PAIR_COLS], U8, name="w_planes_first", align_bytes=64)
+        w_planes_rest = keep.tile([P, PASSES, COLS - PAIR_COLS], U8, name="w_planes_rest", align_bytes=64)
 
-        def scale_window(g, wc):
-            if wc < PAIR_COLS:
-                return planes0[:, g, wc : wc + WIN]
-            return planes_rest[:, g, wc - PAIR_COLS : wc - PAIR_COLS + WIN]
+        def zero_planes(planes):
+            nc.vector.memset(planes[:].rearrange("p g n -> p (g n)").bitcast(I32), 0)
 
-        def load_w_scales(dst, col0, col1):
-            for first in range(8):
-                p = 32 * (first // 4) + first % 4
+        def load_w_planes(planes, first_col, end_col):
+            for q in range(8):
+                p = 32 * (q // 4) + q % 4
                 nc.sync.dma_start(
-                    out=dst[p:P:64, :, :].bitcast(I32),
-                    in_=w_scales[:, first:16:8, col0:col1].rearrange("g q n -> q g n").bitcast(I32),
+                    out=planes[p:P:64, :, :].bitcast(I32),
+                    in_=w_scales[:, q:16:8, first_col:end_col].rearrange("g q n -> q g n").bitcast(I32),
                 )
 
-        tiles = {}
-        state = {"next": 0, "live": 0, "banks_used": 0}
+        def w_plane_window(g, win):
+            if win < PAIR_COLS:
+                return w_planes_first[:, g, win : win + WINDOW]
+            return w_planes_rest[:, g, win - PAIR_COLS : win - PAIR_COLS + WINDOW]
 
-        def load_unit(u):
-            c0, width, gs = units[u]
-            nb = 2 * width
-            t = wpool.tile([P, TILE_BYTES], U8, name="wt", tag="wt", align_bytes=64)
-            if len(gs) == 1:
+        code_tiles = {}
+        count = {"loaded": 0, "live": 0, "banks": 0}
+
+        def load_units(limit):
+            while count["loaded"] < len(units) and count["live"] < limit:
+                first_col, width, group = units[count["loaded"]]
+                row = 2 * width
+                tile = code_pool.tile([P, UNIT_BYTES], U8, name="codes", tag="codes", align_bytes=64)
                 nc.sync.dma_start(
-                    out=t[:, 0:nb].bitcast(I32),
-                    in_=w_words[gs[0], :, 2 * c0 : 2 * c0 + nb].bitcast(I32),
+                    out=tile[:, 0 : len(group) * row].rearrange("p (g n) -> p g n", g=len(group)).bitcast(I32),
+                    in_=w_words[group[0] : group[-1] + 1, :, 2 * first_col : 2 * first_col + row]
+                    .rearrange("g p n -> p g n").bitcast(I32),
                 )
-            else:
-                nc.sync.dma_start(
-                    out=t[:, 0 : len(gs) * nb].rearrange("p (g n) -> p g n", g=len(gs)).bitcast(I32),
-                    in_=w_words[gs[0] : gs[-1] + 1, :, 2 * c0 : 2 * c0 + nb].rearrange("g p n -> p g n").bitcast(I32),
-                )
-            tiles[u] = t
+                code_tiles[count["loaded"]] = tile
+                count["loaded"] += 1
+                count["live"] += 1
 
-        def top_up(limit):
-            while state["next"] < len(units) and state["live"] < limit:
-                load_unit(state["next"])
-                state["next"] += 1
-                state["live"] += 1
-
-        top_up(2)
-        nc.vector.memset(planes0[:].rearrange("p g n -> p (g n)").bitcast(I32), 0)
-        nc.vector.memset(xs[:].rearrange("p g n -> p (g n)").bitcast(I32), 0)
-        load_w_scales(planes0, 0, PAIR_COLS)
-        nc.sync.dma_start(out=xc[:].bitcast(I32), in_=x_words.rearrange("g p n -> p g n").bitcast(I32))
+        load_units(2)
+        zero_planes(w_planes_first)
+        zero_planes(x_planes)
+        load_w_planes(w_planes_first, 0, PAIR_COLS)
+        for g0, g1 in ((0, 3), (3, 5), (5, PASSES)):
+            nc.sync.dma_start(out=x_codes[:, g0:g1, :].bitcast(I32),
+                              in_=x_words[g0:g1].rearrange("g p n -> p g n").bitcast(I32))
         for r in range(4):
-            nc.sync.dma_start(
-                out=xs[r:P:32, :, :].bitcast(I32),
-                in_=x_scales[:, r:16:4, :].rearrange("g q n -> q g n").bitcast(I32),
-            )
-        top_up(G)
+            nc.sync.dma_start(out=x_planes[r:P:32, :, :].bitcast(I32),
+                              in_=x_scales[:, r:16:4, :].rearrange("g q n -> q g n").bitcast(I32))
+        load_units(PASSES)
 
-        pos_i = keep.tile([P, 1], I32, name="pos_i")
-        nc.gpsimd.iota(pos_i[:], pattern=[[0, 1]], base=0, channel_multiplier=1)
-        pos = keep.tile([P, 1], F32, name="pos")
-        nc.vector.tensor_copy(out=pos[:], in_=pos_i[:])
+        position_int = keep.tile([P, 1], I32, name="position_int")
+        nc.gpsimd.iota(position_int[:], pattern=[[0, 1]], base=0, channel_multiplier=1)
+        position = keep.tile([P, 1], F32, name="position")
+        nc.vector.tensor_copy(out=position[:], in_=position_int[:])
         eps = keep.tile([P, 1], F32, name="eps")
         nc.vector.memset(eps[:], EPS)
         freq = keep.tile([P, HALF], F32, name="freq")
         nc.vector.memset(freq[:, 0:1], 1.0)
-        n = 1
-        while n < HALF:
-            m = min(n, HALF - n)
-            nc.vector.tensor_scalar(out=freq[:, n : n + m], in0=freq[:, 0:m],
-                                    scalar1=ROPE_BASE ** (-2.0 * n / DH), scalar2=None, op0=ALU.mult)
-            n *= 2
-        ang = keep.tile([P, DH], F32, name="ang")
-        nc.vector.tensor_scalar(out=ang[:, 0:HALF], in0=freq[:], scalar1=pos[:], scalar2=0.5 * PI,
+        filled = 1
+        while filled < HALF:
+            more = min(filled, HALF - filled)
+            nc.vector.tensor_scalar(out=freq[:, filled : filled + more], in0=freq[:, 0:more],
+                                    scalar1=ROPE_BASE ** (-2.0 * filled / SEGMENT), scalar2=None, op0=ALU.mult)
+            filled += more
+        angle = keep.tile([P, SEGMENT], F32, name="angle")
+        nc.vector.tensor_scalar(out=angle[:, 0:HALF], in0=freq[:], scalar1=position[:], scalar2=0.5 * PI,
                                 op0=ALU.mult, op1=ALU.add)
-        nc.vector.tensor_scalar(out=ang[:, HALF:DH], in0=freq[:], scalar1=pos[:], scalar2=None, op0=ALU.mult)
-        turns_i = keep.tile([P, DH], I32, name="turns_i")
-        nc.vector.tensor_scalar(out=turns_i[:], in0=ang[:], scalar1=0.5 / PI, scalar2=None, op0=ALU.mult)
-        turns = keep.tile([P, DH], F32, name="turns")
-        nc.vector.tensor_copy(out=turns[:], in_=turns_i[:])
-        red1 = keep.tile([P, DH], F32, name="red1")
-        nc.vector.scalar_tensor_tensor(out=red1[:], in0=turns[:], scalar=-TWO_PI_HI, in1=ang[:], op0=ALU.mult, op1=ALU.add)
-        red2 = keep.tile([P, DH], F32, name="red2")
-        nc.vector.scalar_tensor_tensor(out=red2[:], in0=turns[:], scalar=-TWO_PI_LO, in1=red1[:], op0=ALU.mult, op1=ALU.add)
-        over = keep.tile([P, DH], F32, name="over")
-        nc.vector.tensor_scalar(out=over[:], in0=red2[:], scalar1=PI, scalar2=None, op0=ALU.is_gt)
-        red3 = keep.tile([P, DH], F32, name="red3")
-        nc.vector.scalar_tensor_tensor(out=red3[:], in0=over[:], scalar=-2.0 * PI, in1=red2[:], op0=ALU.mult, op1=ALU.add)
-        under = keep.tile([P, DH], F32, name="under")
-        nc.vector.tensor_scalar(out=under[:], in0=red3[:], scalar1=-PI, scalar2=None, op0=ALU.is_lt)
-        red4 = keep.tile([P, DH], F32, name="red4")
-        nc.vector.scalar_tensor_tensor(out=red4[:], in0=under[:], scalar=2.0 * PI, in1=red3[:], op0=ALU.mult, op1=ALU.add)
-        cos2 = keep.tile([P, DH], F32, name="cos2")
-        sin2 = keep.tile([P, DH], F32, name="sin2")
-        nc.scalar.activation(out=cos2[:, 0:HALF], in_=red4[:, 0:HALF], func=ACT.Sin)
-        nc.scalar.activation(out=cos2[:, HALF:DH], in_=red4[:, 0:HALF], func=ACT.Sin)
-        nc.scalar.activation(out=sin2[:, 0:HALF], in_=red4[:, HALF:DH], func=ACT.Sin)
-        nc.scalar.activation(out=sin2[:, HALF:DH], in_=red4[:, HALF:DH], func=ACT.Sin, scale=-1.0)
-        warm = keep.tile([P, 1], F32, name="warm")
-        nc.scalar.activation(out=warm[:], in_=eps[:], func=ACT.Sqrt)
-        junk = keep.tile([P, DH], F32, name="junk")
+        nc.vector.tensor_scalar(out=angle[:, HALF:SEGMENT], in0=freq[:], scalar1=position[:], scalar2=None,
+                                op0=ALU.mult)
+        turns_int = keep.tile([P, SEGMENT], I32, name="turns_int")
+        nc.vector.tensor_scalar(out=turns_int[:], in0=angle[:], scalar1=0.5 / PI, scalar2=None, op0=ALU.mult)
+        turns = keep.tile([P, SEGMENT], F32, name="turns")
+        nc.vector.tensor_copy(out=turns[:], in_=turns_int[:])
+        less_high = keep.tile([P, SEGMENT], F32, name="less_high")
+        nc.vector.scalar_tensor_tensor(out=less_high[:], in0=turns[:], scalar=-TWO_PI_HIGH, in1=angle[:],
+                                       op0=ALU.mult, op1=ALU.add)
+        less_turns = keep.tile([P, SEGMENT], F32, name="less_turns")
+        nc.vector.scalar_tensor_tensor(out=less_turns[:], in0=turns[:], scalar=-TWO_PI_LOW, in1=less_high[:],
+                                       op0=ALU.mult, op1=ALU.add)
+        above_pi = keep.tile([P, SEGMENT], F32, name="above_pi")
+        nc.vector.tensor_scalar(out=above_pi[:], in0=less_turns[:], scalar1=PI, scalar2=None, op0=ALU.is_gt)
+        reduced = keep.tile([P, SEGMENT], F32, name="reduced")
+        nc.vector.scalar_tensor_tensor(out=reduced[:], in0=above_pi[:], scalar=-2.0 * PI, in1=less_turns[:],
+                                       op0=ALU.mult, op1=ALU.add)
+        cos_cos = keep.tile([P, SEGMENT], F32, name="cos_cos")
+        sin_minus_sin = keep.tile([P, SEGMENT], F32, name="sin_minus_sin")
+        nc.scalar.activation(out=cos_cos[:, 0:HALF], in_=reduced[:, 0:HALF], func=FUNC.Sin)
+        nc.scalar.activation(out=cos_cos[:, HALF:SEGMENT], in_=reduced[:, 0:HALF], func=FUNC.Sin)
+        nc.scalar.activation(out=sin_minus_sin[:, 0:HALF], in_=reduced[:, HALF:SEGMENT], func=FUNC.Sin)
+        nc.scalar.activation(out=sin_minus_sin[:, HALF:SEGMENT], in_=reduced[:, HALF:SEGMENT], func=FUNC.Sin,
+                             scale=-1.0)
+        table_change = keep.tile([P, 1], F32, name="table_change")
+        nc.scalar.activation(out=table_change[:], in_=eps[:], func=FUNC.Sqrt)
+        squares = keep.tile([P, SEGMENT], F32, name="squares")
 
-        nc.vector.memset(planes_rest[:].rearrange("p g n -> p (g n)").bitcast(I32), 0)
-        load_w_scales(planes_rest, PAIR_COLS, COLS)
+        zero_planes(w_planes_rest)
+        load_w_planes(w_planes_rest, PAIR_COLS, COLS)
 
-        free_banks = list(range(8))
+        free_banks = list(range(PSUM_BANKS))
 
-        for j, (segs, where) in enumerate(jobs):
-            banks = []
-            for seg in segs:
-                b = free_banks[state["banks_used"]]
-                state["banks_used"] += 1
-                acc = psum.tile([P, WIN], F32, name="bank%d" % b, tag="bank%d" % b)
-                banks.append((b, acc))
-            for g in range(G):
-                u, slot = where[g]
-                c0, width, gs = units[u]
-                for (kind, h, wc, off), (b, acc) in zip(segs, banks):
-                    b0 = 2 * (slot * width + wc - c0)
+        for j, (segments, where) in enumerate(jobs):
+            accs = []
+            for segment in segments:
+                bank = free_banks[count["banks"]]
+                count["banks"] += 1
+                acc = psum.tile([P, WINDOW], F32, name="bank%d" % bank, tag="bank%d" % bank)
+                accs.append((bank, acc))
+            for g in range(PASSES):
+                unit, place = where[g]
+                first_col, width, group = units[unit]
+                for (kind, head, win, valid), (bank, acc) in zip(segments, accs):
+                    byte = 2 * (place * width + win - first_col)
                     nc.tensor.matmul_mx(
                         out=acc[:],
-                        lhsT=xc[:, g, :].bitcast(FP4X4),
-                        lhsT_scale=xs[:, g, :],
-                        rhs=tiles[u][:, b0 : b0 + 2 * WIN].bitcast(FP4X4),
-                        rhs_scale=scale_window(g, wc),
+                        lhsT=x_codes[:, g, :].bitcast(FP4X4),
+                        lhsT_scale=x_planes[:, g, :],
+                        rhs=code_tiles[unit][:, byte : byte + 2 * WINDOW].bitcast(FP4X4),
+                        rhs_scale=w_plane_window(g, win),
                         start=(g == 0),
-                        stop=(g == G - 1),
+                        stop=(g == PASSES - 1),
                     )
-                if last_use[u] == (j, g):
-                    state["live"] -= 1
+                if last_use[unit] == (j, g):
+                    count["live"] -= 1
                     if j > 0:
-                        top_up(W_BUFS)
+                        load_units(LIVE_UNITS)
 
             heads = {}
-            for kind, h, wc, off in segs:
-                heads.setdefault(kind, []).append(h)
-            otiles = {}
+            for kind, head, win, valid in segments:
+                heads.setdefault(kind, []).append(head)
+            out_tiles = {}
             for kind in heads:
-                ot = outp.tile([P, 2 * DH], F32, name="o" + kind, tag="o" + kind)
-                otiles[kind] = ot
+                out_tile = out_pool.tile([P, 2 * SEGMENT], F32, name="out_" + kind, tag="out_" + kind)
+                out_tiles[kind] = out_tile
 
-            rstds = {}
-            for (kind, h, wc, off), (b, acc) in zip(segs, banks):
-                dst = otiles[kind][:, (h - heads[kind][0]) * DH : (h - heads[kind][0] + 1) * DH]
+            def out_slice(kind, head):
+                col = (head - heads[kind][0]) * SEGMENT
+                return out_tiles[kind][:, col : col + SEGMENT]
+
+            rms = {}
+            for (kind, head, win, valid), (bank, acc) in zip(segments, accs):
                 if kind == "v":
-                    nc.scalar.copy(out=dst, in_=acc[:, off : off + DH])
+                    nc.scalar.copy(out=out_slice(kind, head), in_=acc[:, valid : valid + SEGMENT])
                 else:
-                    ss = small.tile([P, 1], F32, name="ss", tag="ss")
-                    nc.scalar.activation(out=junk[:], in_=acc[:, off : off + DH], func=ACT.Square, accum_out=ss[:])
-                    std = small.tile([P, 1], F32, name="std", tag="std")
-                    nc.scalar.activation(out=std[:], in_=ss[:], func=ACT.Sqrt, bias=eps[:], scale=1.0 / DH)
-                    rstds[(kind, h)] = std
-            prods = []
-            for (kind, h, wc, off), (b, acc) in zip(segs, banks):
+                    sum_squares = stat_pool.tile([P, 1], F32, name="sum_squares", tag="sum_squares")
+                    nc.scalar.activation(out=squares[:], in_=acc[:, valid : valid + SEGMENT], func=FUNC.Square,
+                                         accum_out=sum_squares[:])
+                    root = stat_pool.tile([P, 1], F32, name="root", tag="root")
+                    nc.scalar.activation(out=root[:], in_=sum_squares[:], func=FUNC.Sqrt, bias=eps[:],
+                                         scale=1.0 / SEGMENT)
+                    rms[(kind, head)] = root
+
+            products = []
+            for (kind, head, win, valid), (bank, acc) in zip(segments, accs):
                 if kind == "v":
                     continue
-                dst = otiles[kind][:, (h - heads[kind][0]) * DH : (h - heads[kind][0] + 1) * DH]
-                rs = small.tile([P, 1], F32, name="rs", tag="rs")
-                nc.vector.reciprocal(out=rs[:], in_=rstds[(kind, h)][:])
-                at = rot.tile([P, DH], F32, name="at", tag="at")
-                bt = rot.tile([P, DH], F32, name="bt", tag="bt")
-                nc.vector.scalar_tensor_tensor(out=at[:], in0=acc[:, off : off + DH], scalar=rs[:], in1=cos2[:],
+                norm = stat_pool.tile([P, 1], F32, name="norm", tag="norm")
+                nc.vector.reciprocal(out=norm[:], in_=rms[(kind, head)][:])
+                straight = product_pool.tile([P, SEGMENT], F32, name="straight", tag="straight")
+                crossed = product_pool.tile([P, SEGMENT], F32, name="crossed", tag="crossed")
+                nc.vector.scalar_tensor_tensor(out=straight[:], in0=acc[:, valid : valid + SEGMENT], scalar=norm[:],
+                                               in1=cos_cos[:], op0=ALU.mult, op1=ALU.mult)
+                nc.vector.scalar_tensor_tensor(out=crossed[:, 0:HALF], in0=acc[:, valid + HALF : valid + SEGMENT],
+                                               scalar=norm[:], in1=sin_minus_sin[:, 0:HALF],
                                                op0=ALU.mult, op1=ALU.mult)
-                nc.vector.scalar_tensor_tensor(out=bt[:, 0:HALF], in0=acc[:, off + HALF : off + DH], scalar=rs[:],
-                                               in1=sin2[:, 0:HALF], op0=ALU.mult, op1=ALU.mult)
-                nc.vector.scalar_tensor_tensor(out=bt[:, HALF:DH], in0=acc[:, off : off + HALF], scalar=rs[:],
-                                               in1=sin2[:, HALF:DH], op0=ALU.mult, op1=ALU.mult)
-                prods.append((dst, at, bt))
-            for dst, at, bt in prods:
-                nc.vector.tensor_tensor(out=dst, in0=at[:], in1=bt[:], op=ALU.add)
-            for want_v in (True, False):
-                for (kind, h, wc, off), (b, acc) in zip(segs, banks):
-                    if (kind == "v") == want_v:
-                        free_banks.append(b)
+                nc.vector.scalar_tensor_tensor(out=crossed[:, HALF:SEGMENT], in0=acc[:, valid : valid + HALF],
+                                               scalar=norm[:], in1=sin_minus_sin[:, HALF:SEGMENT],
+                                               op0=ALU.mult, op1=ALU.mult)
+                products.append((out_slice(kind, head), straight, crossed))
+            for result, straight, crossed in products:
+                nc.vector.tensor_tensor(out=result, in0=straight[:], in1=crossed[:], op=ALU.add)
+
+            for v_banks in (True, False):
+                for (kind, head, win, valid), (bank, acc) in zip(segments, accs):
+                    if (kind == "v") == v_banks:
+                        free_banks.append(bank)
+
             if j == 0:
-                for kind, cuts in (("v", (0, DH, DH + HALF, 2 * DH)), ("q", (0, DH, 2 * DH)), ("k", (0, DH, 2 * DH))):
-                    for lo, hi in zip(cuts[:-1], cuts[1:]):
-                        nc.sync.dma_start(out=outs[kind][:, lo:hi], in_=otiles[kind][:, lo:hi])
-                top_up(W_BUFS)
+                for kind, cuts in (("v", (0, SEGMENT, SEGMENT + HALF, 2 * SEGMENT)),
+                                   ("q", (0, SEGMENT, 2 * SEGMENT)), ("k", (0, SEGMENT, 2 * SEGMENT))):
+                    for low, high in zip(cuts[:-1], cuts[1:]):
+                        nc.sync.dma_start(out=outs[kind][:, low:high], in_=out_tiles[kind][:, low:high])
+                load_units(LIVE_UNITS)
             else:
                 for kind in heads:
-                    h0 = heads[kind][0]
-                    n_h = len(heads[kind])
-                    queue = nc.gpsimd if n_h == 2 else nc.sync
-                    queue.dma_start(out=outs[kind][:, h0 * DH : (h0 + n_h) * DH], in_=otiles[kind][:, 0 : n_h * DH])
+                    out_col = heads[kind][0] * SEGMENT
+                    n_cols = len(heads[kind]) * SEGMENT
+                    queue = nc.gpsimd if len(heads[kind]) == 2 else nc.sync
+                    queue.dma_start(out=outs[kind][:, out_col : out_col + n_cols], in_=out_tiles[kind][:, 0:n_cols])

@@ -22,6 +22,7 @@ WINDOW = 512
 UNIT_BYTES = 2 * PAIR_COLS
 LIVE_UNITS = 16
 PSUM_BANKS = 8
+EARLY = 3
 EPS = 1e-6
 ROPE_BASE = 10000.0
 
@@ -43,7 +44,7 @@ def make_plan():
     units = []
     jobs = []
 
-    def add_job(first_col, width, pass_groups, parts):
+    def add_job(first_col, width, pass_groups, parts, lags):
         where = {}
         for group in pass_groups:
             for place, g in enumerate(group):
@@ -53,15 +54,16 @@ def make_plan():
         for kind, head in parts:
             win, valid = window_of(head * HEAD_COLS + SEGMENT_COL[kind], first_col, first_col + width)
             segments.append((kind, head, win, valid))
-        jobs.append((tuple(segments), where))
+        jobs.append((tuple(segments), where, lags))
 
     one_by_one = tuple((g,) for g in range(PASSES))
     for a in (0, 2, 4):
         add_job(a * HEAD_COLS, PAIR_COLS, one_by_one,
-                (("q", a), ("k", a), ("v", a), ("v", a + 1), ("q", a + 1), ("k", a + 1)))
-    add_job(6 * HEAD_COLS, HEAD_COLS, ((0, 1), (2, 3), (4, 5), (6,)), (("q", 6), ("k", 6), ("v", 6)))
-    add_job(7 * HEAD_COLS, 2 * SEGMENT, ((0, 1, 2), (3, 4, 5), (6,)), (("q", 7), ("k", 7)))
-    add_job(COLS - WINDOW, WINDOW, ((0, 1, 2, 3), (4, 5), (6,)), (("v", 7),))
+                (("v", a), ("v", a + 1), ("q", a), ("k", a), ("q", a + 1), ("k", a + 1)),
+                (0, 0, 0, 0, 0, 0) if a == 0 else (0, 0, 1, 1, 2, 2))
+    add_job(6 * HEAD_COLS, HEAD_COLS, ((0, 1), (2, 3), (4, 5), (6,)), (("q", 6), ("k", 6), ("v", 6)), (0, 0, 0))
+    add_job(7 * HEAD_COLS, 2 * SEGMENT, ((0, 1, 2), (3, 4, 5), (6,)), (("q", 7), ("k", 7)), (0, 0))
+    add_job(COLS - WINDOW, WINDOW, ((0, 1, 2, 3), (4, 5), (6,)), (("v", 7),), (0,))
     return units, jobs
 
 
@@ -69,7 +71,7 @@ def tile_mixerdiffattention_pa_kernel(tc, x_words, x_scales, w_words, w_scales, 
     nc = tc.nc
     units, jobs = make_plan()
     last_use = {}
-    for j, (segments, where) in enumerate(jobs):
+    for j, (segments, where, lags) in enumerate(jobs):
         for g in range(PASSES):
             last_use[where[g][0]] = (j, g)
     outs = {
@@ -89,24 +91,24 @@ def tile_mixerdiffattention_pa_kernel(tc, x_words, x_scales, w_words, w_scales, 
 
         x_codes = keep.tile([P, PASSES, 2 * P], U8, name="x_codes", align_bytes=64)
         x_planes = keep.tile([P, PASSES, P], U8, name="x_planes", align_bytes=64)
-        w_planes_first = keep.tile([P, PASSES, PAIR_COLS], U8, name="w_planes_first", align_bytes=64)
-        w_planes_rest = keep.tile([P, PASSES, COLS - PAIR_COLS], U8, name="w_planes_rest", align_bytes=64)
+        w_planes_early = keep.tile([P, EARLY, COLS], U8, name="w_planes_early", align_bytes=64)
+        w_planes_late = keep.tile([P, PASSES - EARLY, COLS], U8, name="w_planes_late", align_bytes=64)
 
         def zero_planes(planes):
             nc.vector.memset(planes[:].rearrange("p g n -> p (g n)").bitcast(I32), 0)
 
-        def load_w_planes(planes, first_col, end_col):
+        def load_w_planes(planes, first_pass, end_pass):
             for q in range(8):
                 p = 32 * (q // 4) + q % 4
                 nc.sync.dma_start(
                     out=planes[p:P:64, :, :].bitcast(I32),
-                    in_=w_scales[:, q:16:8, first_col:end_col].rearrange("g q n -> q g n").bitcast(I32),
+                    in_=w_scales[first_pass:end_pass, q:16:8, :].rearrange("g q n -> q g n").bitcast(I32),
                 )
 
         def w_plane_window(g, win):
-            if win < PAIR_COLS:
-                return w_planes_first[:, g, win : win + WINDOW]
-            return w_planes_rest[:, g, win - PAIR_COLS : win - PAIR_COLS + WINDOW]
+            if g < EARLY:
+                return w_planes_early[:, g, win : win + WINDOW]
+            return w_planes_late[:, g - EARLY, win : win + WINDOW]
 
         code_tiles = {}
         count = {"loaded": 0, "live": 0, "banks": 0}
@@ -125,17 +127,22 @@ def tile_mixerdiffattention_pa_kernel(tc, x_words, x_scales, w_words, w_scales, 
                 count["loaded"] += 1
                 count["live"] += 1
 
-        load_units(2)
-        zero_planes(w_planes_first)
         zero_planes(x_planes)
-        load_w_planes(w_planes_first, 0, PAIR_COLS)
-        for g0, g1 in ((0, 3), (3, 5), (5, PASSES)):
-            nc.sync.dma_start(out=x_codes[:, g0:g1, :].bitcast(I32),
-                              in_=x_words[g0:g1].rearrange("g p n -> p g n").bitcast(I32))
+        zero_planes(w_planes_early)
+        zero_planes(w_planes_late)
+        nc.sync.dma_start(out=x_codes[:, 0:EARLY, :].bitcast(I32),
+                          in_=x_words[0:EARLY].rearrange("g p n -> p g n").bitcast(I32))
         for r in range(4):
             nc.sync.dma_start(out=x_planes[r:P:32, :, :].bitcast(I32),
                               in_=x_scales[:, r:16:4, :].rearrange("g q n -> q g n").bitcast(I32))
-        load_units(PASSES)
+        load_units(EARLY)
+        load_w_planes(w_planes_early, 0, EARLY)
+        load_w_planes(w_planes_late, EARLY, PASSES)
+        for g in range(EARLY, PASSES):
+            cuts = (0, P, 2 * P) if g < PASSES - 1 else (0, 2 * P)
+            for low, high in zip(cuts[:-1], cuts[1:]):
+                nc.sync.dma_start(out=x_codes[:, g, low:high].bitcast(I32), in_=x_words[g, :, low:high].bitcast(I32))
+        load_units(LIVE_UNITS)
 
         position_int = keep.tile([P, 1], I32, name="position_int")
         nc.gpsimd.iota(position_int[:], pattern=[[0, 1]], base=0, channel_multiplier=1)
@@ -182,36 +189,37 @@ def tile_mixerdiffattention_pa_kernel(tc, x_words, x_scales, w_words, w_scales, 
         nc.scalar.activation(out=table_change[:], in_=eps[:], func=FUNC.Sqrt)
         squares = keep.tile([P, SEGMENT], F32, name="squares")
 
-        zero_planes(w_planes_rest)
-        load_w_planes(w_planes_rest, PAIR_COLS, COLS)
 
         free_banks = list(range(PSUM_BANKS))
 
-        for j, (segments, where) in enumerate(jobs):
+        for j, (segments, where, lags) in enumerate(jobs):
             accs = []
             for segment in segments:
                 bank = free_banks[count["banks"]]
                 count["banks"] += 1
                 acc = psum.tile([P, WINDOW], F32, name="bank%d" % bank, tag="bank%d" % bank)
                 accs.append((bank, acc))
-            for g in range(PASSES):
+            n_seg = len(segments)
+            order = [(i, step - lags[i]) for step in range(PASSES + max(lags)) for i in range(n_seg)
+                     if 0 <= step - lags[i] < PASSES]
+            for i, g in order:
                 unit, place = where[g]
                 first_col, width, group = units[unit]
-                for (kind, head, win, valid), (bank, acc) in zip(segments, accs):
-                    byte = 2 * (place * width + win - first_col)
-                    nc.tensor.matmul_mx(
-                        out=acc[:],
-                        lhsT=x_codes[:, g, :].bitcast(FP4X4),
-                        lhsT_scale=x_planes[:, g, :],
-                        rhs=code_tiles[unit][:, byte : byte + 2 * WINDOW].bitcast(FP4X4),
-                        rhs_scale=w_plane_window(g, win),
-                        start=(g == 0),
-                        stop=(g == PASSES - 1),
-                    )
-                if last_use[unit] == (j, g):
+                kind, head, win, valid = segments[i]
+                bank, acc = accs[i]
+                byte = 2 * (place * width + win - first_col)
+                nc.tensor.matmul_mx(
+                    out=acc[:],
+                    lhsT=x_codes[:, g, :].bitcast(FP4X4),
+                    lhsT_scale=x_planes[:, g, :],
+                    rhs=code_tiles[unit][:, byte : byte + 2 * WINDOW].bitcast(FP4X4),
+                    rhs_scale=w_plane_window(g, win),
+                    start=(g == 0),
+                    stop=(g == PASSES - 1),
+                )
+                if i == n_seg - 1 and last_use[unit] == (j, g):
                     count["live"] -= 1
-                    if j > 0:
-                        load_units(LIVE_UNITS)
+                    load_units(LIVE_UNITS)
 
             heads = {}
             for kind, head, win, valid in segments:
@@ -263,15 +271,8 @@ def tile_mixerdiffattention_pa_kernel(tc, x_words, x_scales, w_words, w_scales, 
                     if (kind == "v") == v_banks:
                         free_banks.append(bank)
 
-            if j == 0:
-                for kind, cuts in (("v", (0, SEGMENT, SEGMENT + HALF, 2 * SEGMENT)),
-                                   ("q", (0, SEGMENT, 2 * SEGMENT)), ("k", (0, SEGMENT, 2 * SEGMENT))):
-                    for low, high in zip(cuts[:-1], cuts[1:]):
-                        nc.sync.dma_start(out=outs[kind][:, low:high], in_=out_tiles[kind][:, low:high])
-                load_units(LIVE_UNITS)
-            else:
-                for kind in heads:
-                    out_col = heads[kind][0] * SEGMENT
-                    n_cols = len(heads[kind]) * SEGMENT
-                    queue = nc.gpsimd if len(heads[kind]) == 2 else nc.sync
-                    queue.dma_start(out=outs[kind][:, out_col : out_col + n_cols], in_=out_tiles[kind][:, 0:n_cols])
+            for kind in heads:
+                out_col = heads[kind][0] * SEGMENT
+                n_cols = len(heads[kind]) * SEGMENT
+                queue = nc.gpsimd if len(heads[kind]) == 2 else nc.sync
+                queue.dma_start(out=outs[kind][:, out_col : out_col + n_cols], in_=out_tiles[kind][:, 0:n_cols])

@@ -86,7 +86,7 @@ def tile_mixerdiffattention_pa_kernel(tc, x_words, x_scales, w_words, w_scales, 
         code_pool = ctx.enter_context(tc.tile_pool(name="code_pool", bufs=LIVE_UNITS))
         stat_pool = ctx.enter_context(tc.tile_pool(name="stat_pool", bufs=8))
         product_pool = ctx.enter_context(tc.tile_pool(name="product_pool", bufs=6))
-        out_pool = ctx.enter_context(tc.tile_pool(name="out_pool", bufs=2))
+        out_pool = ctx.enter_context(tc.tile_pool(name="out_pool", bufs=3))
         psum = ctx.enter_context(tc.psum_pool(name="psum", bufs=1))
 
         x_codes = keep.tile([P, PASSES, 2 * P], U8, name="x_codes", align_bytes=64)
@@ -274,5 +274,5 @@ def tile_mixerdiffattention_pa_kernel(tc, x_words, x_scales, w_words, w_scales, 
             for kind in heads:
                 out_col = heads[kind][0] * SEGMENT
                 n_cols = len(heads[kind]) * SEGMENT
-                queue = nc.gpsimd if len(heads[kind]) == 2 else nc.sync
+                queue = nc.gpsimd if j < 2 else nc.sync
                 queue.dma_start(out=outs[kind][:, out_col : out_col + n_cols], in_=out_tiles[kind][:, 0:n_cols])

@@ -139,7 +139,7 @@ def tile_mixerdiffattention_pa_kernel(tc, x_words, x_scales, w_words, w_scales, 
         load_w_planes(w_planes_early, 0, EARLY)
         load_w_planes(w_planes_late, EARLY, PASSES)
         for g in range(EARLY, PASSES):
-            cuts = (0, P, 2 * P) if g < PASSES - 1 else (0, 2 * P)
+            cuts = (0, P, 2 * P) if g < PASSES - 2 else (0, 2 * P)
             for low, high in zip(cuts[:-1], cuts[1:]):
                 nc.sync.dma_start(out=x_codes[:, g, low:high].bitcast(I32), in_=x_words[g, :, low:high].bitcast(I32))
         load_units(LIVE_UNITS)

@@ -190,6 +190,7 @@ def tile_mixerdiffattention_pa_kernel(tc, x_words, x_scales, w_words, w_scales, 
         squares = keep.tile([P, SEGMENT], F32, name="squares")
 
 
+        pending = []
         free_banks = list(range(PSUM_BANKS))
 
         for j, (segments, where, lags) in enumerate(jobs):
@@ -220,6 +221,10 @@ def tile_mixerdiffattention_pa_kernel(tc, x_words, x_scales, w_words, w_scales, 
                 if i == n_seg - 1 and last_use[unit] == (j, g):
                     count["live"] -= 1
                     load_units(LIVE_UNITS)
+                    if g == PASSES // 2:
+                        for out_ap, in_ap in pending:
+                            nc.sync.dma_start(out=out_ap, in_=in_ap)
+                        pending.clear()
 
             heads = {}
             for kind, head, win, valid in segments:
@@ -274,5 +279,8 @@ def tile_mixerdiffattention_pa_kernel(tc, x_words, x_scales, w_words, w_scales, 
             for kind in heads:
                 out_col = heads[kind][0] * SEGMENT
                 n_cols = len(heads[kind]) * SEGMENT
-                queue = nc.gpsimd if j < 2 else nc.sync
-                queue.dma_start(out=outs[kind][:, out_col : out_col + n_cols], in_=out_tiles[kind][:, 0:n_cols])
+                pending.append((outs[kind][:, out_col : out_col + n_cols], out_tiles[kind][:, 0:n_cols]))
+            if j >= 2:
+                for out_ap, in_ap in pending:
+                    nc.sync.dma_start(out=out_ap, in_=in_ap)
+                pending.clear()

@@ -22,7 +22,7 @@ WINDOW = 512
 UNIT_BYTES = 2 * PAIR_COLS
 LIVE_UNITS = 16
 PSUM_BANKS = 8
-EARLY = 3
+EARLY = 4
 EPS = 1e-6
 ROPE_BASE = 10000.0
 
@@ -132,14 +132,14 @@ def tile_mixerdiffattention_pa_kernel(tc, x_words, x_scales, w_words, w_scales, 
         zero_planes(w_planes_late)
         nc.sync.dma_start(out=x_codes[:, 0:EARLY, :].bitcast(I32),
                           in_=x_words[0:EARLY].rearrange("g p n -> p g n").bitcast(I32))
+        load_units(EARLY)
         for r in range(4):
             nc.sync.dma_start(out=x_planes[r:P:32, :, :].bitcast(I32),
                               in_=x_scales[:, r:16:4, :].rearrange("g q n -> q g n").bitcast(I32))
-        load_units(EARLY)
         load_w_planes(w_planes_early, 0, EARLY)
         load_w_planes(w_planes_late, EARLY, PASSES)
         for g in range(EARLY, PASSES):
-            cuts = (0, P, 2 * P) if g < PASSES - 2 else (0, 2 * P)
+            cuts = (0, P, 2 * P)
             for low, high in zip(cuts[:-1], cuts[1:]):
                 nc.sync.dma_start(out=x_codes[:, g, low:high].bitcast(I32), in_=x_words[g, :, low:high].bitcast(I32))
         load_units(LIVE_UNITS)

from contextlib import ExitStack

import concourse.mybir as mybir

F32 = mybir.dt.float32
I32 = mybir.dt.int32
U8 = mybir.dt.uint8
FP4X4 = mybir.dt.float4_e2m1fn_x4
ALU = mybir.AluOpType
FUNC = mybir.ActivationFunctionType

P = 128
PASSES = 7
HEADS = 8
SEGMENT = 448
HALF = SEGMENT // 2
SEGMENT_COL = {"q": 0, "k": SEGMENT, "v": 2 * SEGMENT}
HEAD_COLS = 3 * SEGMENT
PAIR_COLS = 2 * HEAD_COLS
COLS = HEADS * HEAD_COLS
WINDOW = 512
UNIT_BYTES = 2 * PAIR_COLS
LIVE_UNITS = 16
PSUM_BANKS = 8
EARLY = 4
EPS = 1e-6
ROPE_BASE = 10000.0

PI = 3.141592653589793
TWO_PI_HIGH = 6.28125
TWO_PI_LOW = 2.0 * PI - TWO_PI_HIGH

FLOPS = 2 * 128 * 3584 * 10752


def window_of(first_col, low, high):
    if first_col + WINDOW <= high:
        return first_col, 0
    assert first_col + SEGMENT - WINDOW >= low
    return first_col + SEGMENT - WINDOW, WINDOW - SEGMENT


def make_plan():
    units = []
    jobs = []

    def add_job(first_col, width, pass_groups, parts, lags):
        where = {}
        for group in pass_groups:
            for place, g in enumerate(group):
                where[g] = (len(units), place)
            units.append((first_col, width, group))
        segments = []
        for kind, head in parts:
            win, valid = window_of(head * HEAD_COLS + SEGMENT_COL[kind], first_col, first_col + width)
            segments.append((kind, head, win, valid))
        jobs.append((tuple(segments), where, lags))

    one_by_one = tuple((g,) for g in range(PASSES))
    for a in (0, 2, 4):
        add_job(a * HEAD_COLS, PAIR_COLS, one_by_one,
                (("v", a), ("v", a + 1), ("q", a), ("k", a), ("q", a + 1), ("k", a + 1)),
                (0, 0, 0, 0, 0, 0) if a == 0 else (0, 0, 1, 1, 2, 2))
    add_job(6 * HEAD_COLS, HEAD_COLS, ((0, 1), (2, 3), (4, 5), (6,)), (("q", 6), ("k", 6), ("v", 6)), (0, 0, 0))
    add_job(7 * HEAD_COLS, 2 * SEGMENT, ((0, 1, 2), (3, 4, 5), (6,)), (("q", 7), ("k", 7)), (0, 0))
    add_job(COLS - WINDOW, WINDOW, ((0, 1, 2, 3), (4, 5), (6,)), (("v", 7),), (0,))
    return units, jobs


def tile_mixerdiffattention_pa_kernel(tc, x_words, x_scales, w_words, w_scales, out_0, out_1, out_2):
    nc = tc.nc
    units, jobs = make_plan()
    last_use = {}
    for j, (segments, where, lags) in enumerate(jobs):
        for g in range(PASSES):
            last_use[where[g][0]] = (j, g)
    outs = {
        "q": out_0.rearrange("b t h d -> (b t) (h d)"),
        "k": out_1.rearrange("b t h d -> (b t) (h d)"),
        "v": out_2.rearrange("b t h d -> (b t) (h d)"),
    }

    with ExitStack() as ctx:
        ctx.enter_context(tc.manual_schedule())
        keep = ctx.enter_context(tc.tile_pool(name="keep", bufs=1))
        code_pool = ctx.enter_context(tc.tile_pool(name="code_pool", bufs=LIVE_UNITS))
        stat_pool = ctx.enter_context(tc.tile_pool(name="stat_pool", bufs=8))
        product_pool = ctx.enter_context(tc.tile_pool(name="product_pool", bufs=6))
        out_pool = ctx.enter_context(tc.tile_pool(name="out_pool", bufs=3))
        psum = ctx.enter_context(tc.psum_pool(name="psum", bufs=1))

        x_codes = keep.tile([P, PASSES, 2 * P], U8, name="x_codes", align_bytes=64)
        x_planes = keep.tile([P, PASSES, P], U8, name="x_planes", align_bytes=64)
        w_planes_early = keep.tile([P, EARLY, COLS], U8, name="w_planes_early", align_bytes=64)
        w_planes_late = keep.tile([P, PASSES - EARLY, COLS], U8, name="w_planes_late", align_bytes=64)

        def zero_planes(planes):
            nc.vector.memset(planes[:].rearrange("p g n -> p (g n)").bitcast(I32), 0)

        def load_w_planes(planes, first_pass, end_pass):
            for q in range(8):
                p = 32 * (q // 4) + q % 4
                nc.sync.dma_start(
                    out=planes[p:P:64, :, :].bitcast(I32),
                    in_=w_scales[first_pass:end_pass, q:16:8, :].rearrange("g q n -> q g n").bitcast(I32),
                )

        def w_plane_window(g, win):
            if g < EARLY:
                return w_planes_early[:, g, win : win + WINDOW]
            return w_planes_late[:, g - EARLY, win : win + WINDOW]

        code_tiles = {}
        count = {"loaded": 0, "live": 0, "banks": 0}

        def load_units(limit):
            while count["loaded"] < len(units) and count["live"] < limit:
                first_col, width, group = units[count["loaded"]]
                row = 2 * width
                tile = code_pool.tile([P, UNIT_BYTES], U8, name="codes", tag="codes", align_bytes=64)
                nc.sync.dma_start(
                    out=tile[:, 0 : len(group) * row].rearrange("p (g n) -> p g n", g=len(group)).bitcast(I32),
                    in_=w_words[group[0] : group[-1] + 1, :, 2 * first_col : 2 * first_col + row]
                    .rearrange("g p n -> p g n").bitcast(I32),
                )
                code_tiles[count["loaded"]] = tile
                count["loaded"] += 1
                count["live"] += 1

        zero_planes(x_planes)
        zero_planes(w_planes_early)
        zero_planes(w_planes_late)
        nc.sync.dma_start(out=x_codes[:, 0:EARLY, :].bitcast(I32),
                          in_=x_words[0:EARLY].rearrange("g p n -> p g n").bitcast(I32))
        load_units(EARLY)
        for r in range(4):
            nc.sync.dma_start(out=x_planes[r:P:32, :, :].bitcast(I32),
                              in_=x_scales[:, r:16:4, :].rearrange("g q n -> q g n").bitcast(I32))
        load_w_planes(w_planes_early, 0, EARLY)
        load_w_planes(w_planes_late, EARLY, PASSES)
        for g in range(EARLY, PASSES):
            cuts = (0, P, 2 * P)
            for low, high in zip(cuts[:-1], cuts[1:]):
                nc.sync.dma_start(out=x_codes[:, g, low:high].bitcast(I32), in_=x_words[g, :, low:high].bitcast(I32))
        load_units(LIVE_UNITS)

        position_int = keep.tile([P, 1], I32, name="position_int")
        nc.gpsimd.iota(position_int[:], pattern=[[0, 1]], base=0, channel_multiplier=1)
        position = keep.tile([P, 1], F32, name="position")
        nc.vector.tensor_copy(out=position[:], in_=position_int[:])
        eps = keep.tile([P, 1], F32, name="eps")
        nc.vector.memset(eps[:], EPS)
        freq = keep.tile([P, HALF], F32, name="freq")
        nc.vector.memset(freq[:, 0:1], 1.0)
        filled = 1
        while filled < HALF:
            more = min(filled, HALF - filled)
            nc.vector.tensor_scalar(out=freq[:, filled : filled + more], in0=freq[:, 0:more],
                                    scalar1=ROPE_BASE ** (-2.0 * filled / SEGMENT), scalar2=None, op0=ALU.mult)
            filled += more
        angle = keep.tile([P, SEGMENT], F32, name="angle")
        nc.vector.tensor_scalar(out=angle[:, 0:HALF], in0=freq[:], scalar1=position[:], scalar2=0.5 * PI,
                                op0=ALU.mult, op1=ALU.add)
        nc.vector.tensor_scalar(out=angle[:, HALF:SEGMENT], in0=freq[:], scalar1=position[:], scalar2=None,
                                op0=ALU.mult)
        turns_int = keep.tile([P, SEGMENT], I32, name="turns_int")
        nc.vector.tensor_scalar(out=turns_int[:], in0=angle[:], scalar1=0.5 / PI, scalar2=None, op0=ALU.mult)
        turns = keep.tile([P, SEGMENT], F32, name="turns")
        nc.vector.tensor_copy(out=turns[:], in_=turns_int[:])
        less_high = keep.tile([P, SEGMENT], F32, name="less_high")
        nc.vector.scalar_tensor_tensor(out=less_high[:], in0=turns[:], scalar=-TWO_PI_HIGH, in1=angle[:],
                                       op0=ALU.mult, op1=ALU.add)
        less_turns = keep.tile([P, SEGMENT], F32, name="less_turns")
        nc.vector.scalar_tensor_tensor(out=less_turns[:], in0=turns[:], scalar=-TWO_PI_LOW, in1=less_high[:],
                                       op0=ALU.mult, op1=ALU.add)
        above_pi = keep.tile([P, SEGMENT], F32, name="above_pi")
        nc.vector.tensor_scalar(out=above_pi[:], in0=less_turns[:], scalar1=PI, scalar2=None, op0=ALU.is_gt)
        reduced = keep.tile([P, SEGMENT], F32, name="reduced")
        nc.vector.scalar_tensor_tensor(out=reduced[:], in0=above_pi[:], scalar=-2.0 * PI, in1=less_turns[:],
                                       op0=ALU.mult, op1=ALU.add)
        cos_cos = keep.tile([P, SEGMENT], F32, name="cos_cos")
        sin_minus_sin = keep.tile([P, SEGMENT], F32, name="sin_minus_sin")
        nc.scalar.activation(out=cos_cos[:, 0:HALF], in_=reduced[:, 0:HALF], func=FUNC.Sin)
        nc.scalar.activation(out=cos_cos[:, HALF:SEGMENT], in_=reduced[:, 0:HALF], func=FUNC.Sin)
        nc.scalar.activation(out=sin_minus_sin[:, 0:HALF], in_=reduced[:, HALF:SEGMENT], func=FUNC.Sin)
        nc.scalar.activation(out=sin_minus_sin[:, HALF:SEGMENT], in_=reduced[:, HALF:SEGMENT], func=FUNC.Sin,
                             scale=-1.0)
        table_change = keep.tile([P, 1], F32, name="table_change")
        nc.scalar.activation(out=table_change[:], in_=eps[:], func=FUNC.Sqrt)
        squares = keep.tile([P, SEGMENT], F32, name="squares")


        pending = []
        free_banks = list(range(PSUM_BANKS))

        for j, (segments, where, lags) in enumerate(jobs):
            accs = []
            for segment in segments:
                bank = free_banks[count["banks"]]
                count["banks"] += 1
                acc = psum.tile([P, WINDOW], F32, name="bank%d" % bank, tag="bank%d" % bank)
                accs.append((bank, acc))
            n_seg = len(segments)
            order = [(i, step - lags[i]) for step in range(PASSES + max(lags)) for i in range(n_seg)
                     if 0 <= step - lags[i] < PASSES]
            for i, g in order:
                unit, place = where[g]
                first_col, width, group = units[unit]
                kind, head, win, valid = segments[i]
                bank, acc = accs[i]
                byte = 2 * (place * width + win - first_col)
                nc.tensor.matmul_mx(
                    out=acc[:],
                    lhsT=x_codes[:, g, :].bitcast(FP4X4),
                    lhsT_scale=x_planes[:, g, :],
                    rhs=code_tiles[unit][:, byte : byte + 2 * WINDOW].bitcast(FP4X4),
                    rhs_scale=w_plane_window(g, win),
                    start=(g == 0),
                    stop=(g == PASSES - 1),
                )
                if i == n_seg - 1 and last_use[unit] == (j, g):
                    count["live"] -= 1
                    load_units(LIVE_UNITS)
                    if g == PASSES // 2:
                        for out_ap, in_ap in pending:
                            nc.sync.dma_start(out=out_ap, in_=in_ap)
                        pending.clear()

            heads = {}
            for kind, head, win, valid in segments:
                heads.setdefault(kind, []).append(head)
            out_tiles = {}
            for kind in heads:
                out_tile = out_pool.tile([P, 2 * SEGMENT], F32, name="out_" + kind, tag="out_" + kind)
                out_tiles[kind] = out_tile

            def out_slice(kind, head):
                col = (head - heads[kind][0]) * SEGMENT
                return out_tiles[kind][:, col : col + SEGMENT]

            rms = {}
            for (kind, head, win, valid), (bank, acc) in zip(segments, accs):
                if kind == "v":
                    nc.scalar.copy(out=out_slice(kind, head), in_=acc[:, valid : valid + SEGMENT])
                else:
                    sum_squares = stat_pool.tile([P, 1], F32, name="sum_squares", tag="sum_squares")
                    nc.scalar.activation(out=squares[:], in_=acc[:, valid : valid + SEGMENT], func=FUNC.Square,
                                         accum_out=sum_squares[:])
                    root = stat_pool.tile([P, 1], F32, name="root", tag="root")
                    nc.scalar.activation(out=root[:], in_=sum_squares[:], func=FUNC.Sqrt, bias=eps[:],
                                         scale=1.0 / SEGMENT)
                    rms[(kind, head)] = root

            products = []
            for (kind, head, win, valid), (bank, acc) in zip(segments, accs):
                if kind == "v":
                    continue
                norm = stat_pool.tile([P, 1], F32, name="norm", tag="norm")
                nc.vector.reciprocal(out=norm[:], in_=rms[(kind, head)][:])
                straight = product_pool.tile([P, SEGMENT], F32, name="straight", tag="straight")
                crossed = product_pool.tile([P, SEGMENT], F32, name="crossed", tag="crossed")
                nc.vector.scalar_tensor_tensor(out=straight[:], in0=acc[:, valid : valid + SEGMENT], scalar=norm[:],
                                               in1=cos_cos[:], op0=ALU.mult, op1=ALU.mult)
                nc.vector.scalar_tensor_tensor(out=crossed[:, 0:HALF], in0=acc[:, valid + HALF : valid + SEGMENT],
                                               scalar=norm[:], in1=sin_minus_sin[:, 0:HALF],
                                               op0=ALU.mult, op1=ALU.mult)
                nc.vector.scalar_tensor_tensor(out=crossed[:, HALF:SEGMENT], in0=acc[:, valid : valid + HALF],
                                               scalar=norm[:], in1=sin_minus_sin[:, HALF:SEGMENT],
                                               op0=ALU.mult, op1=ALU.mult)
                products.append((out_slice(kind, head), straight, crossed))
            for result, straight, crossed in products:
                nc.vector.tensor_tensor(out=result, in0=straight[:], in1=crossed[:], op=ALU.add)

            for v_banks in (True, False):
                for (kind, head, win, valid), (bank, acc) in zip(segments, accs):
                    if (kind == "v") == v_banks:
                        free_banks.append(bank)

            for kind in heads:
                out_col = heads[kind][0] * SEGMENT
                n_cols = len(heads[kind]) * SEGMENT
                pending.append((outs[kind][:, out_col : out_col + n_cols], out_tiles[kind][:, 0:n_cols]))
            if j >= 2:
                for out_ap, in_ap in pending:
                    nc.sync.dma_start(out=out_ap, in_=in_ap)
                pending.clear()
